import numpy as np
import ml_dtypes


def mxq(x, axis, fmt="e4m3"):
    dtype, down = {"e4m3": (ml_dtypes.float8_e4m3fn, 7), "e5m2": (ml_dtypes.float8_e5m2, 14)}[fmt]
    v = np.moveaxis(np.asarray(x, np.float32).astype(ml_dtypes.bfloat16).astype(np.float64), axis, -1)
    blocks = v.reshape(v.shape[:-1] + (-1, 32))
    amax = np.abs(blocks).max(-1, keepdims=True)
    byte = np.maximum(np.where(amax > 0, np.frexp(amax)[1] - 1 + 127, 0) - down, 1)
    scale = np.exp2(byte - 127.0)
    codes = (blocks / scale).astype(np.float32).astype(dtype).astype(np.float64)
    return np.moveaxis((codes * scale).reshape(v.shape), -1, axis)


WIDE = False


def mx_kscale(k):
    if not WIDE:
        return np.ones(k)
    levels = np.array([10, -10, 5, -5, 0])
    a = np.random.permutation(np.resize(levels, k // 512 * 4)).reshape(k // 512, 4)
    idx = np.arange(k)
    return np.exp2(a[idx // 512, idx % 128 // 32])


BF16 = ml_dtypes.bfloat16


def bf(x):
    return np.asarray(x, np.float32).astype(BF16)


def f64(x):
    return np.asarray(x).astype(np.float64)


B, S, IN, OUT, GS = 4, 2048, 1024, 128, 128
G = IN // GS


def setup_inputs():
    s = mx_kscale(IN)
    m = (1.0 / s).reshape(G, GS).min(axis=1)
    return {"quantized_x": bf(np.random.standard_normal((B, S, IN)) * s),
            "scales_x": bf(0.25 + 0.75 * np.random.random((B, S, 1))),
            "weight": bf(np.random.standard_normal((OUT, IN)) / s),
            "weight_scales": bf((0.5 + np.random.random((OUT, G))) / np.sqrt(IN)),
            "offset_w": bf(np.random.standard_normal((OUT, G)) * m)}


def reference(quantized_x, scales_x, weight, weight_scales, offset_w):
    x = f64(quantized_x) * f64(scales_x)
    Wq = f64(weight).reshape(OUT, G, GS)
    W = (Wq - f64(offset_w)[:, :, None]) * f64(weight_scales)[:, :, None]
    W = W.reshape(OUT, IN)
    return mxq(x, 2, "e4m3") @ mxq(W, 1, "e4m3").T

@@ -1,0 +1,180 @@
+import concourse.mybir as mybir
+from concourse.masks import make_identity
+
+FP8X4 = mybir.dt.float8_e4m3fn_x4
+BF16 = mybir.dt.bfloat16
+F32 = mybir.dt.float32
+U32 = mybir.dt.uint32
+U8 = mybir.dt.uint8
+ALU = mybir.AluOpType
+
+P = 128
+TOKENS = 8192
+FEATURES = 1024
+OUTS = 128
+TILES = TOKENS // P
+UNITS = TILES // 2
+K_PASS = 512
+PASSES = FEATURES // K_PASS
+WORDS = K_PASS // 2
+GROUPS = 8
+CHUNKS = [2, 2] + [4] * 15
+FLOPS = 2 * TOKENS * FEATURES * OUTS
+
+
+def tile_quarotfp16linear_t_kernel(tc, quantized_x, scales_x, weight, weight_scales, offset_w, out):
+    nc = tc.nc
+    x_view = quantized_x.flatten_outer_dims().rearrange("(p t) k -> p t k", t=TILES)
+    s_view = scales_x.flatten_outer_dims().rearrange("(p t) o -> p (t o)", t=TILES)
+    out_view = out.flatten_outer_dims().rearrange("(p t) o -> p t o", t=TILES)
+
+    with tc.tile_pool(name="keep", bufs=1) as keep, tc.tile_pool(name="work", bufs=3) as work, tc.tile_pool(
+        name="res", bufs=4
+    ) as res, tc.psum_pool(name="xt", bufs=2) as xt_pool, tc.psum_pool(name="acc", bufs=2) as acc_pool, tc.psum_pool(
+        name="setup", bufs=2
+    ) as setup_pool, tc.manual_schedule():
+        s_sb = keep.tile([P, TILES], BF16)
+        nc.sync.dma_start(out=s_sb[:], in_=s_view)
+        w_sb = keep.tile([P, FEATURES], BF16)
+        nc.scalar.dma_start(out=w_sb[:], in_=weight)
+        off_sb = keep.tile([P, GROUPS], BF16)
+        nc.scalar.dma_start(out=off_sb[:], in_=offset_w)
+        ws_sb = keep.tile([P, GROUPS], BF16)
+        nc.scalar.dma_start(out=ws_sb[:], in_=weight_scales)
+        x_words = []
+        first = 0
+        for c, n in enumerate(CHUNKS):
+            xc = keep.tile([P, n, FEATURES], BF16, name="xc%d" % c)
+            nc.sync.dma_start(out=xc[:], in_=x_view[:, first : first + n, :])
+            words = xc[:].rearrange("p n k -> p (n k)").bitcast(F32)
+            x_words.extend([words[:, i * (FEATURES // 2) : (i + 1) * (FEATURES // 2)] for i in range(n)])
+            first += n
+
+        ident_f32 = keep.tile([P, P], F32)
+        make_identity(nc, ident_f32[:])
+        ident_bf = keep.tile([P, P], BF16)
+        make_identity(nc, ident_bf[:])
+
+        s_pair = keep.tile([P, TILES, 2], BF16)
+        nc.vector.tensor_copy(out=s_pair[:], in_=s_sb[:].unsqueeze(2).to_broadcast([P, TILES, 2]))
+        s_words = s_pair[:].rearrange("p t e -> p (t e)").bitcast(F32)
+        s2 = keep.tile([P, TILES * P], F32)
+
+        def spread_scales(t0):
+            bank = setup_pool.tile([P, 4, P], F32, tag="setup")
+            for i in range(4):
+                nc.tensor.transpose(
+                    out=bank[:, i, :], in_=s_words[:, t0 + i : t0 + i + 1].to_broadcast([P, P]), identity=ident_f32[:]
+                )
+            nc.scalar.copy(out=s2[:, t0 * P : (t0 + 4) * P], in_=bank[:].rearrange("p i r -> p (i r)"))
+
+        spread_scales(0)
+
+        off32 = keep.tile([P, GROUPS], F32)
+        nc.vector.tensor_copy(out=off32[:], in_=off_sb[:])
+        ws32 = keep.tile([P, GROUPS], F32)
+        nc.vector.tensor_copy(out=ws32[:], in_=ws_sb[:])
+        w_deq = keep.tile([P, PASSES, 2, 2, P], BF16)
+        for q in range(GROUPS):
+            g, u, h = q // 4, (q // 2) % 2, q % 2
+            nc.vector.tensor_scalar(
+                out=w_deq[:, g, u, :, 64 * h : 64 * h + 64],
+                in0=w_sb[:, q * P : (q + 1) * P].rearrange("p (m e) -> p e m", e=2),
+                scalar1=off32[:, q : q + 1],
+                scalar2=ws32[:, q : q + 1],
+                op0=ALU.subtract,
+                op1=ALU.mult,
+            )
+        wt = setup_pool.tile([P, PASSES * 4, OUTS], BF16, tag="setup")
+        for g in range(PASSES):
+            for u in range(2):
+                for e in range(2):
+                    nc.tensor.transpose(out=wt[:, g * 4 + 2 * u + e, :], in_=w_deq[:, g, u, e, :], identity=ident_bf[:])
+        w_grouped = keep.tile([P, PASSES, OUTS, 4], BF16, align_bytes=64)
+        nc.scalar.copy(out=w_grouped[:], in_=wt[:].rearrange("p (g t) o -> p g o t", g=PASSES))
+        w_codes = keep.tile([P, PASSES * OUTS], U32, align_bytes=64)
+        w_scl = keep.tile([P, PASSES * OUTS], U8, align_bytes=64)
+
+        def transposes(unit):
+            banks = []
+            for g in range(PASSES):
+                bank = xt_pool.tile([P, 2, 2 * P], F32, name="xt%d" % g)
+                for j in range(2):
+                    for u in range(2):
+                        lo = g * WORDS + u * P
+                        nc.tensor.transpose(
+                            out=bank[:, u, j * P : (j + 1) * P],
+                            in_=x_words[2 * unit + j][:, lo : lo + P],
+                            identity=ident_f32[:],
+                        )
+                banks.append(bank)
+            return banks
+
+        def scale_out(unit, banks):
+            grouped = work.tile([P, PASSES, 2 * P * 4], BF16, align_bytes=64)
+            s_unit = (
+                s2[:, 2 * unit * P : (2 * unit + 2) * P]
+                .bitcast(BF16)
+                .rearrange("p (c e) -> p c e", e=2)
+                .unsqueeze(2)
+                .to_broadcast([P, 2 * P, 2, 2])
+            )
+            for g in range(PASSES):
+                nc.vector.tensor_tensor(
+                    out=grouped[:, g, :].rearrange("p (c u e) -> p c u e", u=2, e=2),
+                    in0=banks[g][:].rearrange("p u c -> p (u c)").bitcast(BF16).rearrange("p (u c e) -> p c u e", u=2, e=2),
+                    in1=s_unit,
+                    op=ALU.mult,
+                )
+            return grouped
+
+        def quantise(grouped):
+            codes = work.tile([P, PASSES * 2 * P], U32, align_bytes=64)
+            scl = work.tile([P, PASSES * 2 * P], U8, align_bytes=64)
+            nc.vector.quantize_mx(out=codes[:].bitcast(FP8X4), scales=scl[:], in_=grouped[:].rearrange("p g c -> p (g c)"))
+            return codes, scl
+
+        def multiply(unit, codes, scl, acc):
+            for j in range(2):
+                slot = (2 * unit + j) % 4
+                for g in range(PASSES):
+                    cols = slice((g * 2 + j) * P, (g * 2 + j + 1) * P)
+                    w_c = slice(g * OUTS, (g + 1) * OUTS)
+                    nc.tensor.matmul_mx(
+                        out=acc[:, slot * OUTS : (slot + 1) * OUTS],
+                        lhsT=codes[:, cols].bitcast(FP8X4),
+                        lhsT_scale=scl[:, cols],
+                        rhs=w_codes[:, w_c].bitcast(FP8X4),
+                        rhs_scale=w_scl[:, w_c],
+                        start=(g == 0),
+                        stop=(g == PASSES - 1),
+                    )
+
+        banks_of = {0: transposes(0), 1: transposes(1)}
+        grouped_of = {}
+        accs = {}
+
+        def finish(unit):
+            codes, scl = quantise(grouped_of[unit])
+            if unit % 2 == 0:
+                acc = acc_pool.tile([P, 4 * OUTS], F32)
+                accs[unit // 2] = acc
+            multiply(unit, codes, scl, accs[unit // 2])
+            if unit % 2 == 1:
+                result = res.tile([P, 4, OUTS], F32)
+                nc.scalar.copy(out=result[:].rearrange("p t o -> p (t o)"), in_=accs[unit // 2][:])
+                nc.scalar.dma_start(out=out_view[:, 2 * unit - 2 : 2 * unit + 2, :], in_=result[:])
+
+        for unit in range(UNITS):
+            grouped_of[unit] = scale_out(unit, banks_of[unit])
+            if unit == 0:
+                nc.vector.quantize_mx(
+                    out=w_codes[:].bitcast(FP8X4), scales=w_scl[:], in_=w_grouped[:].rearrange("p g o t -> p (g o t)")
+                )
+            else:
+                finish(unit - 1)
+            if unit % 2 == 0 and unit + 2 < UNITS:
+                spread_scales(2 * (unit + 2))
+            if unit + 2 < UNITS:
+                banks_of[unit + 2] = transposes(unit + 2)
+        finish(UNITS - 1)

@@ -19,6 +19,7 @@ PASSES = FEATURES // K_PASS
 WORDS = K_PASS // 2
 GROUPS = 8
 CHUNKS = [2, 2] + [4] * 15
+DUMMIES = 2
 FLOPS = 2 * TOKENS * FEATURES * OUTS
 
 
@@ -31,8 +32,8 @@ def tile_quarotfp16linear_t_kernel(tc, quantized_x, scales_x, weight, weight_sca
     with tc.tile_pool(name="keep", bufs=1) as keep, tc.tile_pool(name="work", bufs=3) as work, tc.tile_pool(
         name="res", bufs=4
     ) as res, tc.psum_pool(name="xt", bufs=2) as xt_pool, tc.psum_pool(name="acc", bufs=2) as acc_pool, tc.psum_pool(
-        name="setup", bufs=2
-    ) as setup_pool, tc.manual_schedule():
+        name="setup", bufs=1
+    ) as setup_pool, tc.psum_pool(name="junk", bufs=1) as junk_pool, tc.manual_schedule():
         s_sb = keep.tile([P, TILES], BF16)
         nc.sync.dma_start(out=s_sb[:], in_=s_view)
         w_sb = keep.tile([P, FEATURES], BF16)
@@ -150,6 +151,20 @@ def tile_quarotfp16linear_t_kernel(tc, quantized_x, scales_x, weight, weight_sca
                         stop=(g == PASSES - 1),
                     )
 
+        junk = junk_pool.tile([P, 4 * P], F32)
+
+        def keep_busy(codes, scl):
+            for d in range(DUMMIES):
+                nc.tensor.matmul_mx(
+                    out=junk[:],
+                    lhsT=codes[:, 0:P].bitcast(FP8X4),
+                    lhsT_scale=scl[:, 0:P],
+                    rhs=codes[:].bitcast(FP8X4),
+                    rhs_scale=scl[:],
+                    start=True,
+                    stop=True,
+                )
+
         banks_of = {0: transposes(0), 1: transposes(1)}
         grouped_of = {}
         accs = {}
@@ -160,6 +175,7 @@ def tile_quarotfp16linear_t_kernel(tc, quantized_x, scales_x, weight, weight_sca
                 acc = acc_pool.tile([P, 4 * OUTS], F32)
                 accs[unit // 2] = acc
             multiply(unit, codes, scl, accs[unit // 2])
+            keep_busy(codes, scl)
             if unit % 2 == 1:
                 result = res.tile([P, 4, OUTS], F32)
                 nc.scalar.copy(out=result[:].rearrange("p t o -> p (t o)"), in_=accs[unit // 2][:])

@@ -29,7 +29,7 @@ def tile_quarotfp16linear_t_kernel(tc, quantized_x, scales_x, weight, weight_sca
     s_view = scales_x.flatten_outer_dims().rearrange("(p t) o -> p (t o)", t=TILES)
     out_view = out.flatten_outer_dims().rearrange("(p t) o -> p t o", t=TILES)
 
-    with tc.tile_pool(name="keep", bufs=1) as keep, tc.tile_pool(name="work", bufs=3) as work, tc.tile_pool(
+    with tc.tile_pool(name="keep", bufs=1) as keep, tc.tile_pool(name="work", bufs=3) as work, tc.tile_pool(name="spread", bufs=3) as spread, tc.tile_pool(
         name="res", bufs=4
     ) as res, tc.psum_pool(name="xt", bufs=2) as xt_pool, tc.psum_pool(name="acc", bufs=2) as acc_pool, tc.psum_pool(
         name="setup", bufs=1
@@ -59,7 +59,7 @@ def tile_quarotfp16linear_t_kernel(tc, quantized_x, scales_x, weight, weight_sca
         s_pair = keep.tile([P, TILES, 2], BF16)
         nc.vector.tensor_copy(out=s_pair[:], in_=s_sb[:].unsqueeze(2).to_broadcast([P, TILES, 2]))
         s_words = s_pair[:].rearrange("p t e -> p (t e)").bitcast(F32)
-        s2 = keep.tile([P, TILES * P], F32)
+        s4_of = {}
 
         def spread_scales(t0):
             bank = setup_pool.tile([P, 4, P], F32, tag="setup")
@@ -67,7 +67,9 @@ def tile_quarotfp16linear_t_kernel(tc, quantized_x, scales_x, weight, weight_sca
                 nc.tensor.transpose(
                     out=bank[:, i, :], in_=s_words[:, t0 + i : t0 + i + 1].to_broadcast([P, P]), identity=ident_f32[:]
                 )
-            nc.scalar.copy(out=s2[:, t0 * P : (t0 + 4) * P], in_=bank[:].rearrange("p i r -> p (i r)"))
+            s4 = spread.tile([P, 4 * P, 2], F32)
+            nc.scalar.copy(out=s4[:], in_=bank[:].rearrange("p i r -> p (i r)").unsqueeze(2).to_broadcast([P, 4 * P, 2]))
+            s4_of[t0] = s4
 
         spread_scales(0)
 
@@ -113,13 +115,8 @@ def tile_quarotfp16linear_t_kernel(tc, quantized_x, scales_x, weight, weight_sca
 
         def scale_out(unit, banks):
             grouped = work.tile([P, PASSES, 2 * P * 4], BF16, align_bytes=64)
-            s_unit = (
-                s2[:, 2 * unit * P : (2 * unit + 2) * P]
-                .bitcast(BF16)
-                .rearrange("p (c e) -> p c e", e=2)
-                .unsqueeze(2)
-                .to_broadcast([P, 2 * P, 2, 2])
-            )
+            half = 2 * P * (unit % 2)
+            s_unit = s4_of[4 * (unit // 2)][:, half : half + 2 * P, :].rearrange("p c u -> p (c u)").bitcast(BF16).rearrange("p (c u e) -> p c u e", u=2, e=2)
             for g in range(PASSES):
                 nc.vector.tensor_tensor(
                     out=grouped[:, g, :].rearrange("p (c u e) -> p c u e", u=2, e=2),

@@ -19,7 +19,7 @@ PASSES = FEATURES // K_PASS
 WORDS = K_PASS // 2
 GROUPS = 8
 CHUNKS = [2, 2] + [4] * 15
-DUMMIES = 2
+DUMMIES = 1
 FLOPS = 2 * TOKENS * FEATURES * OUTS
 
 
@@ -29,7 +29,7 @@ def tile_quarotfp16linear_t_kernel(tc, quantized_x, scales_x, weight, weight_sca
     s_view = scales_x.flatten_outer_dims().rearrange("(p t) o -> p (t o)", t=TILES)
     out_view = out.flatten_outer_dims().rearrange("(p t) o -> p t o", t=TILES)
 
-    with tc.tile_pool(name="keep", bufs=1) as keep, tc.tile_pool(name="work", bufs=3) as work, tc.tile_pool(name="spread", bufs=3) as spread, tc.tile_pool(
+    with tc.tile_pool(name="keep", bufs=1) as keep, tc.tile_pool(name="work", bufs=3) as work, tc.tile_pool(name="spread", bufs=4) as spread, tc.tile_pool(
         name="res", bufs=4
     ) as res, tc.psum_pool(name="xt", bufs=2) as xt_pool, tc.psum_pool(name="acc", bufs=2) as acc_pool, tc.psum_pool(
         name="setup", bufs=1
@@ -72,6 +72,7 @@ def tile_quarotfp16linear_t_kernel(tc, quantized_x, scales_x, weight, weight_sca
             s4_of[t0] = s4
 
         spread_scales(0)
+        spread_scales(4)
 
         off32 = keep.tile([P, GROUPS], F32)
         nc.vector.tensor_copy(out=off32[:], in_=off_sb[:])
@@ -150,8 +151,8 @@ def tile_quarotfp16linear_t_kernel(tc, quantized_x, scales_x, weight, weight_sca
 
         junk = junk_pool.tile([P, 4 * P], F32)
 
-        def keep_busy(codes, scl):
-            for d in range(DUMMIES):
+        def keep_busy(unit, codes, scl):
+            for d in range(2 if unit < 4 else DUMMIES):
                 nc.tensor.matmul_mx(
                     out=junk[:],
                     lhsT=codes[:, 0:P].bitcast(FP8X4),
@@ -172,7 +173,7 @@ def tile_quarotfp16linear_t_kernel(tc, quantized_x, scales_x, weight, weight_sca
                 acc = acc_pool.tile([P, 4 * OUTS], F32)
                 accs[unit // 2] = acc
             multiply(unit, codes, scl, accs[unit // 2])
-            keep_busy(codes, scl)
+            keep_busy(unit, codes, scl)
             if unit % 2 == 1:
                 result = res.tile([P, 4, OUTS], F32)
                 nc.scalar.copy(out=result[:].rearrange("p t o -> p (t o)"), in_=accs[unit // 2][:])
@@ -180,14 +181,14 @@ def tile_quarotfp16linear_t_kernel(tc, quantized_x, scales_x, weight, weight_sca
 
         for unit in range(UNITS):
             grouped_of[unit] = scale_out(unit, banks_of[unit])
+            if unit + 2 < UNITS:
+                banks_of[unit + 2] = transposes(unit + 2)
+            if unit % 2 == 0 and unit + 4 < UNITS:
+                spread_scales(2 * (unit + 4))
             if unit == 0:
                 nc.vector.quantize_mx(
                     out=w_codes[:].bitcast(FP8X4), scales=w_scl[:], in_=w_grouped[:].rearrange("p g o t -> p (g o t)")
                 )
             else:
                 finish(unit - 1)
-            if unit % 2 == 0 and unit + 2 < UNITS:
-                spread_scales(2 * (unit + 2))
-            if unit + 2 < UNITS:
-                banks_of[unit + 2] = transposes(unit + 2)
         finish(UNITS - 1)

@@ -13,13 +13,12 @@ TOKENS = 8192
 FEATURES = 1024
 OUTS = 128
 TILES = TOKENS // P
-UNITS = TILES // 2
+PERIODS = TILES // 8
+PAIRS = 3 * PERIODS
 K_PASS = 512
 PASSES = FEATURES // K_PASS
 WORDS = K_PASS // 2
 GROUPS = 8
-CHUNKS = [2, 2] + [4] * 15
-DUMMIES = 1
 FLOPS = 2 * TOKENS * FEATURES * OUTS
 
 
@@ -29,11 +28,13 @@ def tile_quarotfp16linear_t_kernel(tc, quantized_x, scales_x, weight, weight_sca
     s_view = scales_x.flatten_outer_dims().rearrange("(p t) o -> p (t o)", t=TILES)
     out_view = out.flatten_outer_dims().rearrange("(p t) o -> p t o", t=TILES)
 
-    with tc.tile_pool(name="keep", bufs=1) as keep, tc.tile_pool(name="work", bufs=3) as work, tc.tile_pool(name="spread", bufs=4) as spread, tc.tile_pool(
-        name="res", bufs=4
-    ) as res, tc.psum_pool(name="xt", bufs=2) as xt_pool, tc.psum_pool(name="acc", bufs=2) as acc_pool, tc.psum_pool(
-        name="setup", bufs=1
-    ) as setup_pool, tc.psum_pool(name="junk", bufs=1) as junk_pool, tc.manual_schedule():
+    with tc.tile_pool(name="keep", bufs=1) as keep, tc.tile_pool(name="spread", bufs=5) as spread, tc.tile_pool(
+        name="work", bufs=3
+    ) as work, tc.tile_pool(name="awork", bufs=2) as awork, tc.tile_pool(name="res", bufs=3) as res, tc.psum_pool(
+        name="xb", bufs=3
+    ) as xb_pool, tc.psum_pool(name="aux", bufs=3) as aux_pool, tc.psum_pool(
+        name="acc", bufs=2
+    ) as acc_pool, tc.manual_schedule():
         s_sb = keep.tile([P, TILES], BF16)
         nc.sync.dma_start(out=s_sb[:], in_=s_view)
         w_sb = keep.tile([P, FEATURES], BF16)
@@ -42,14 +43,17 @@ def tile_quarotfp16linear_t_kernel(tc, quantized_x, scales_x, weight, weight_sca
         nc.scalar.dma_start(out=off_sb[:], in_=offset_w)
         ws_sb = keep.tile([P, GROUPS], BF16)
         nc.scalar.dma_start(out=ws_sb[:], in_=weight_scales)
-        x_words = []
-        first = 0
-        for c, n in enumerate(CHUNKS):
+        x_bf = {}
+        x_words = {}
+        chunks = [[0, 1], [2, 3], [6, 7], [4, 5]] + [[t, t + 1, t + 2, t + 3] for t in range(8, TILES, 4)]
+        for c, tiles in enumerate(chunks):
+            n = len(tiles)
             xc = keep.tile([P, n, FEATURES], BF16, name="xc%d" % c)
-            nc.sync.dma_start(out=xc[:], in_=x_view[:, first : first + n, :])
+            nc.sync.dma_start(out=xc[:], in_=x_view[:, tiles[0] : tiles[0] + n, :])
             words = xc[:].rearrange("p n k -> p (n k)").bitcast(F32)
-            x_words.extend([words[:, i * (FEATURES // 2) : (i + 1) * (FEATURES // 2)] for i in range(n)])
-            first += n
+            for i, t in enumerate(tiles):
+                x_bf[t] = xc[:, i, :]
+                x_words[t] = words[:, i * (FEATURES // 2) : (i + 1) * (FEATURES // 2)]
 
         ident_f32 = keep.tile([P, P], F32)
         make_identity(nc, ident_f32[:])
@@ -59,136 +63,204 @@ def tile_quarotfp16linear_t_kernel(tc, quantized_x, scales_x, weight, weight_sca
         s_pair = keep.tile([P, TILES, 2], BF16)
         nc.vector.tensor_copy(out=s_pair[:], in_=s_sb[:].unsqueeze(2).to_broadcast([P, TILES, 2]))
         s_words = s_pair[:].rearrange("p t e -> p (t e)").bitcast(F32)
+        s32 = keep.tile([P, TILES], F32)
+        nc.vector.tensor_copy(out=s32[:], in_=s_sb[:])
+
+        def first_tile(k):
+            return 8 * (k // 3) + 2 * (k % 3)
+
         s4_of = {}
 
-        def spread_scales(t0):
-            bank = setup_pool.tile([P, 4, P], F32, tag="setup")
-            for i in range(4):
-                nc.tensor.transpose(
-                    out=bank[:, i, :], in_=s_words[:, t0 + i : t0 + i + 1].to_broadcast([P, P]), identity=ident_f32[:]
-                )
-            s4 = spread.tile([P, 4 * P, 2], F32)
-            nc.scalar.copy(out=s4[:], in_=bank[:].rearrange("p i r -> p (i r)").unsqueeze(2).to_broadcast([P, 4 * P, 2]))
-            s4_of[t0] = s4
-
-        spread_scales(0)
-        spread_scales(4)
+        def spread_scales(k):
+            if k >= PAIRS:
+                return
+            bank = aux_pool.tile([P, 2, P], F32, tag="aux")
+            for i in range(2):
+                t = first_tile(k) + i
+                nc.tensor.transpose(out=bank[:, i, :], in_=s_words[:, t : t + 1].to_broadcast([P, P]), identity=ident_f32[:])
+            s4 = spread.tile([P, 2 * P, 2], F32)
+            nc.scalar.copy(out=s4[:], in_=bank[:].rearrange("p i r -> p (i r)").unsqueeze(2).to_broadcast([P, 2 * P, 2]))
+            s4_of[k] = s4
 
         off32 = keep.tile([P, GROUPS], F32)
         nc.vector.tensor_copy(out=off32[:], in_=off_sb[:])
         ws32 = keep.tile([P, GROUPS], F32)
         nc.vector.tensor_copy(out=ws32[:], in_=ws_sb[:])
-        w_deq = keep.tile([P, PASSES, 2, 2, P], BF16)
+        noff32 = keep.tile([P, GROUPS], F32)
+        nc.vector.tensor_scalar(out=noff32[:], in0=off_sb[:], scalar1=-1.0, scalar2=None, op0=ALU.mult)
+        w_deq_b = keep.tile([P, PASSES, 2, 2, P], BF16)
         for q in range(GROUPS):
             g, u, h = q // 4, (q // 2) % 2, q % 2
             nc.vector.tensor_scalar(
-                out=w_deq[:, g, u, :, 64 * h : 64 * h + 64],
+                out=w_deq_b[:, g, u, :, 64 * h : 64 * h + 64],
                 in0=w_sb[:, q * P : (q + 1) * P].rearrange("p (m e) -> p e m", e=2),
                 scalar1=off32[:, q : q + 1],
                 scalar2=ws32[:, q : q + 1],
                 op0=ALU.subtract,
                 op1=ALU.mult,
             )
-        wt = setup_pool.tile([P, PASSES * 4, OUTS], BF16, tag="setup")
-        for g in range(PASSES):
-            for u in range(2):
-                for e in range(2):
-                    nc.tensor.transpose(out=wt[:, g * 4 + 2 * u + e, :], in_=w_deq[:, g, u, e, :], identity=ident_bf[:])
-        w_grouped = keep.tile([P, PASSES, OUTS, 4], BF16, align_bytes=64)
-        nc.scalar.copy(out=w_grouped[:], in_=wt[:].rearrange("p (g t) o -> p g o t", g=PASSES))
-        w_codes = keep.tile([P, PASSES * OUTS], U32, align_bytes=64)
-        w_scl = keep.tile([P, PASSES * OUTS], U8, align_bytes=64)
+        w_deq_a = keep.tile([P, FEATURES], BF16)
+        for q in range(GROUPS):
+            nc.gpsimd.tensor_scalar(
+                out=w_deq_a[:, q * P : (q + 1) * P],
+                in0=w_sb[:, q * P : (q + 1) * P],
+                scalar1=noff32[:, q : q + 1],
+                scalar2=ws32[:, q : q + 1],
+                op0=ALU.add,
+                op1=ALU.mult,
+            )
+        w_grouped = {}
+        w_codes = {}
+        w_scl = {}
 
-        def transposes(unit):
-            banks = []
+        def w_transposes(way):
+            wt = aux_pool.tile([P, PASSES * 4, OUTS], BF16, tag="aux")
             for g in range(PASSES):
-                bank = xt_pool.tile([P, 2, 2 * P], F32, name="xt%d" % g)
-                for j in range(2):
-                    for u in range(2):
-                        lo = g * WORDS + u * P
-                        nc.tensor.transpose(
-                            out=bank[:, u, j * P : (j + 1) * P],
-                            in_=x_words[2 * unit + j][:, lo : lo + P],
-                            identity=ident_f32[:],
-                        )
-                banks.append(bank)
-            return banks
+                for t in range(4):
+                    src = w_deq_b[:, g, t // 2, t % 2, :] if way == "b" else w_deq_a[:, g * K_PASS + t * P : g * K_PASS + (t + 1) * P]
+                    nc.tensor.transpose(out=wt[:, g * 4 + t, :], in_=src, identity=ident_bf[:])
+            wg = keep.tile([P, PASSES, OUTS, 4], BF16, name="wg_" + way, align_bytes=64)
+            nc.scalar.copy(out=wg[:], in_=wt[:].rearrange("p (g t) o -> p g o t", g=PASSES))
+            w_grouped[way] = wg
 
-        def scale_out(unit, banks):
-            grouped = work.tile([P, PASSES, 2 * P * 4], BF16, align_bytes=64)
-            half = 2 * P * (unit % 2)
-            s_unit = s4_of[4 * (unit // 2)][:, half : half + 2 * P, :].rearrange("p c u -> p (c u)").bitcast(BF16).rearrange("p (c u e) -> p c u e", u=2, e=2)
-            for g in range(PASSES):
-                nc.vector.tensor_tensor(
-                    out=grouped[:, g, :].rearrange("p (c u e) -> p c u e", u=2, e=2),
-                    in0=banks[g][:].rearrange("p u c -> p (u c)").bitcast(BF16).rearrange("p (u c e) -> p c u e", u=2, e=2),
-                    in1=s_unit,
-                    op=ALU.mult,
-                )
-            return grouped
+        def w_quantise(way):
+            wc = keep.tile([P, PASSES * OUTS], U32, name="wc_" + way, align_bytes=64)
+            wsc = keep.tile([P, PASSES * OUTS], U8, name="wsc_" + way, align_bytes=64)
+            nc.vector.quantize_mx(
+                out=wc[:].bitcast(FP8X4), scales=wsc[:], in_=w_grouped[way][:].rearrange("p g o t -> p (g o t)")
+            )
+            w_codes[way] = wc
+            w_scl[way] = wsc
 
-        def quantise(grouped):
-            codes = work.tile([P, PASSES * 2 * P], U32, align_bytes=64)
-            scl = work.tile([P, PASSES * 2 * P], U8, align_bytes=64)
-            nc.vector.quantize_mx(out=codes[:].bitcast(FP8X4), scales=scl[:], in_=grouped[:].rearrange("p g c -> p (g c)"))
-            return codes, scl
+        banks = {}
 
-        def multiply(unit, codes, scl, acc):
+        def b_transposes(i):
+            k, g = i // 2, i % 2
+            if k >= PAIRS:
+                return
+            bank = xb_pool.tile([P, 2, 2 * P], F32, tag="xb")
             for j in range(2):
-                slot = (2 * unit + j) % 4
-                for g in range(PASSES):
-                    cols = slice((g * 2 + j) * P, (g * 2 + j + 1) * P)
-                    w_c = slice(g * OUTS, (g + 1) * OUTS)
-                    nc.tensor.matmul_mx(
-                        out=acc[:, slot * OUTS : (slot + 1) * OUTS],
-                        lhsT=codes[:, cols].bitcast(FP8X4),
-                        lhsT_scale=scl[:, cols],
-                        rhs=w_codes[:, w_c].bitcast(FP8X4),
-                        rhs_scale=w_scl[:, w_c],
-                        start=(g == 0),
-                        stop=(g == PASSES - 1),
+                for u in range(2):
+                    lo = g * WORDS + u * P
+                    nc.tensor.transpose(
+                        out=bank[:, u, j * P : (j + 1) * P],
+                        in_=x_words[first_tile(k) + j][:, lo : lo + P],
+                        identity=ident_f32[:],
                     )
+            banks[i] = bank
 
-        junk = junk_pool.tile([P, 4 * P], F32)
-
-        def keep_busy(unit, codes, scl):
-            for d in range(2 if unit < 4 else DUMMIES):
-                nc.tensor.matmul_mx(
-                    out=junk[:],
-                    lhsT=codes[:, 0:P].bitcast(FP8X4),
-                    lhsT_scale=scl[:, 0:P],
-                    rhs=codes[:].bitcast(FP8X4),
-                    rhs_scale=scl[:],
-                    start=True,
-                    stop=True,
-                )
-
-        banks_of = {0: transposes(0), 1: transposes(1)}
         grouped_of = {}
+
+        def b_scale(k, g):
+            if g == 0:
+                grouped = work.tile([P, PASSES, 2 * P * 4], BF16, align_bytes=64)
+                grouped_of[k] = grouped
+            nc.vector.tensor_tensor(
+                out=grouped_of[k][:, g, :].rearrange("p (c u e) -> p c u e", u=2, e=2),
+                in0=banks[2 * k + g][:].rearrange("p u c -> p (u c)").bitcast(BF16).rearrange("p (u c e) -> p c u e", u=2, e=2),
+                in1=s4_of[k][:].rearrange("p c u -> p (c u)").bitcast(BF16).rearrange("p (c u e) -> p c u e", u=2, e=2),
+                op=ALU.mult,
+            )
+
         accs = {}
 
-        def finish(unit):
-            codes, scl = quantise(grouped_of[unit])
-            if unit % 2 == 0:
+        def multiply(tile, codes, scl, col0, step, way):
+            if tile // 4 not in accs:
                 acc = acc_pool.tile([P, 4 * OUTS], F32)
-                accs[unit // 2] = acc
-            multiply(unit, codes, scl, accs[unit // 2])
-            keep_busy(unit, codes, scl)
-            if unit % 2 == 1:
-                result = res.tile([P, 4, OUTS], F32)
-                nc.scalar.copy(out=result[:].rearrange("p t o -> p (t o)"), in_=accs[unit // 2][:])
-                nc.scalar.dma_start(out=out_view[:, 2 * unit - 2 : 2 * unit + 2, :], in_=result[:])
-
-        for unit in range(UNITS):
-            grouped_of[unit] = scale_out(unit, banks_of[unit])
-            if unit + 2 < UNITS:
-                banks_of[unit + 2] = transposes(unit + 2)
-            if unit % 2 == 0 and unit + 4 < UNITS:
-                spread_scales(2 * (unit + 4))
-            if unit == 0:
-                nc.vector.quantize_mx(
-                    out=w_codes[:].bitcast(FP8X4), scales=w_scl[:], in_=w_grouped[:].rearrange("p g o t -> p (g o t)")
+                accs[tile // 4] = acc
+            slot = tile % 4
+            for g in range(PASSES):
+                cols = slice(col0 + g * step, col0 + g * step + P)
+                w_c = slice(g * OUTS, (g + 1) * OUTS)
+                nc.tensor.matmul_mx(
+                    out=accs[tile // 4][:, slot * OUTS : (slot + 1) * OUTS],
+                    lhsT=codes[:, cols].bitcast(FP8X4),
+                    lhsT_scale=scl[:, cols],
+                    rhs=w_codes[way][:, w_c].bitcast(FP8X4),
+                    rhs_scale=w_scl[way][:, w_c],
+                    start=(g == 0),
+                    stop=(g == PASSES - 1),
                 )
-            else:
-                finish(unit - 1)
-        finish(UNITS - 1)
+
+        def b_finish(k):
+            codes = work.tile([P, PASSES * 2 * P], U32, align_bytes=64)
+            scl = work.tile([P, PASSES * 2 * P], U8, align_bytes=64)
+            nc.vector.quantize_mx(out=codes[:].bitcast(FP8X4), scales=scl[:], in_=grouped_of[k][:].rearrange("p g c -> p (g c)"))
+            for j in range(2):
+                multiply(first_tile(k) + j, codes, scl, j * P, 2 * P, "b")
+
+        xs_of = {}
+        ga_of = {}
+
+        def a_scale(n, a):
+            if n >= PERIODS:
+                return
+            t = 8 * n + 6 + a
+            xs = awork.tile([P, FEATURES], BF16, name="xs%d" % a)
+            nc.vector.tensor_scalar_mul(out=xs[:], in0=x_bf[t], scalar1=s32[:, t : t + 1])
+            xs_of[(n, a)] = xs
+
+        def a_transposes(n, a):
+            bank = aux_pool.tile([P, PASSES * 4, P], BF16, tag="aux")
+            for i in range(PASSES * 4):
+                nc.tensor.transpose(out=bank[:, i, :], in_=xs_of[(n, a)][:, i * P : (i + 1) * P], identity=ident_bf[:])
+            if a == 0:
+                ga = awork.tile([P, 2, PASSES, P, 4], BF16, align_bytes=64)
+                ga_of[n] = ga
+            nc.scalar.copy(out=ga_of[n][:, a, :, :, :], in_=bank[:].rearrange("p (g t) r -> p g r t", g=PASSES))
+
+        def a_finish(n):
+            codes_a = awork.tile([P, 2 * PASSES * P], U32, align_bytes=64)
+            scl_a = awork.tile([P, 2 * PASSES * P], U8, align_bytes=64)
+            nc.vector.quantize_mx(
+                out=codes_a[:].bitcast(FP8X4), scales=scl_a[:], in_=ga_of[n][:].rearrange("p a g r t -> p (a g r t)")
+            )
+            for a in range(2):
+                multiply(8 * n + 6 + a, codes_a, scl_a, a * PASSES * P, P, "a")
+
+        def send(bank):
+            result = res.tile([P, 4, OUTS], F32)
+            nc.scalar.copy(out=result[:].rearrange("p t o -> p (t o)"), in_=accs[bank][:])
+            nc.scalar.dma_start(out=out_view[:, 4 * bank : 4 * bank + 4, :], in_=result[:])
+
+        spread_scales(0)
+        spread_scales(1)
+        spread_scales(2)
+        b_transposes(0)
+        b_transposes(1)
+        w_transposes("b")
+        b_transposes(2)
+        for k in range(PAIRS):
+            n, j = k // 3, k % 3
+            b_scale(k, 0)
+            b_transposes(2 * k + 3)
+            b_scale(k, 1)
+            b_transposes(2 * k + 4)
+            if k == 0:
+                w_transposes("a")
+            if k == 1:
+                a_scale(0, 0)
+                a_scale(0, 1)
+            if (n >= 1 and j == 0) or k == 1:
+                a_transposes(n, 0)
+            if (n >= 1 and j == 1) or k == 2:
+                a_transposes(n, 1)
+            spread_scales(k + 3)
+            if k == 1:
+                w_quantise("b")
+            if k == 2:
+                w_quantise("a")
+            if k >= 1:
+                b_finish(k - 1)
+            if j == 0 and n >= 1:
+                a_finish(n - 1)
+            if j == 2:
+                a_scale(n + 1, 0)
+                a_scale(n + 1, 1)
+            if j == 2:
+                send(2 * n)
+            if j == 0 and n >= 1:
+                send(2 * n - 1)
+        a_finish(PERIODS - 1)
+        b_finish(PAIRS - 1)
+        send(2 * PERIODS - 1)

@@ -28,9 +28,9 @@ def tile_quarotfp16linear_t_kernel(tc, quantized_x, scales_x, weight, weight_sca
     s_view = scales_x.flatten_outer_dims().rearrange("(p t) o -> p (t o)", t=TILES)
     out_view = out.flatten_outer_dims().rearrange("(p t) o -> p t o", t=TILES)
 
-    with tc.tile_pool(name="keep", bufs=1) as keep, tc.tile_pool(name="spread", bufs=5) as spread, tc.tile_pool(
+    with tc.tile_pool(name="keep", bufs=1) as keep, tc.tile_pool(name="spread", bufs=4) as spread, tc.tile_pool(
         name="work", bufs=3
-    ) as work, tc.tile_pool(name="awork", bufs=2) as awork, tc.tile_pool(name="res", bufs=3) as res, tc.psum_pool(
+    ) as work, tc.tile_pool(name="awork", bufs=2) as awork, tc.tile_pool(name="res", bufs=16) as res, tc.psum_pool(
         name="xb", bufs=3
     ) as xb_pool, tc.psum_pool(name="aux", bufs=3) as aux_pool, tc.psum_pool(
         name="acc", bufs=2
@@ -45,7 +45,8 @@ def tile_quarotfp16linear_t_kernel(tc, quantized_x, scales_x, weight, weight_sca
         nc.scalar.dma_start(out=ws_sb[:], in_=weight_scales)
         x_bf = {}
         x_words = {}
-        chunks = [[0, 1], [2, 3], [6, 7], [4, 5]] + [[t, t + 1, t + 2, t + 3] for t in range(8, TILES, 4)]
+        chunks = [[0, 1], [2, 3], [6, 7], [4, 5], [8, 9], [14, 15], [10, 11], [12, 13]]
+        chunks = chunks + [[t, t + 1, t + 2, t + 3] for t in range(16, TILES, 4)]
         for c, tiles in enumerate(chunks):
             n = len(tiles)
             xc = keep.tile([P, n, FEATURES], BF16, name="xc%d" % c)
@@ -69,18 +70,18 @@ def tile_quarotfp16linear_t_kernel(tc, quantized_x, scales_x, weight, weight_sca
         def first_tile(k):
             return 8 * (k // 3) + 2 * (k % 3)
 
-        s4_of = {}
+        s2_of = {}
 
-        def spread_scales(k):
-            if k >= PAIRS:
+        def spread_scales(q):
+            if 2 * q >= PAIRS:
                 return
-            bank = aux_pool.tile([P, 2, P], F32, tag="aux")
-            for i in range(2):
-                t = first_tile(k) + i
+            bank = aux_pool.tile([P, 4, P], F32, tag="aux")
+            for i in range(4):
+                t = first_tile(2 * q + i // 2) + i % 2
                 nc.tensor.transpose(out=bank[:, i, :], in_=s_words[:, t : t + 1].to_broadcast([P, P]), identity=ident_f32[:])
-            s4 = spread.tile([P, 2 * P, 2], F32)
-            nc.scalar.copy(out=s4[:], in_=bank[:].rearrange("p i r -> p (i r)").unsqueeze(2).to_broadcast([P, 2 * P, 2]))
-            s4_of[k] = s4
+            s2 = spread.tile([P, 4 * P], F32)
+            nc.scalar.copy(out=s2[:], in_=bank[:].rearrange("p i r -> p (i r)"))
+            s2_of[q] = s2
 
         off32 = keep.tile([P, GROUPS], F32)
         nc.vector.tensor_copy(out=off32[:], in_=off_sb[:])
@@ -158,7 +159,11 @@ def tile_quarotfp16linear_t_kernel(tc, quantized_x, scales_x, weight, weight_sca
             nc.vector.tensor_tensor(
                 out=grouped_of[k][:, g, :].rearrange("p (c u e) -> p c u e", u=2, e=2),
                 in0=banks[2 * k + g][:].rearrange("p u c -> p (u c)").bitcast(BF16).rearrange("p (u c e) -> p c u e", u=2, e=2),
-                in1=s4_of[k][:].rearrange("p c u -> p (c u)").bitcast(BF16).rearrange("p (c u e) -> p c u e", u=2, e=2),
+                in1=s2_of[k // 2][:, (k % 2) * 2 * P : (k % 2 + 1) * 2 * P]
+                .bitcast(BF16)
+                .rearrange("p (c e) -> p c e", e=2)
+                .unsqueeze(2)
+                .to_broadcast([P, 2 * P, 2, 2]),
                 op=ALU.mult,
             )
 
@@ -221,11 +226,10 @@ def tile_quarotfp16linear_t_kernel(tc, quantized_x, scales_x, weight, weight_sca
         def send(bank):
             result = res.tile([P, 4, OUTS], F32)
             nc.scalar.copy(out=result[:].rearrange("p t o -> p (t o)"), in_=accs[bank][:])
-            nc.scalar.dma_start(out=out_view[:, 4 * bank : 4 * bank + 4, :], in_=result[:])
+            nc.sync.dma_start(out=out_view[:, 4 * bank : 4 * bank + 4, :], in_=result[:])
 
         spread_scales(0)
         spread_scales(1)
-        spread_scales(2)
         b_transposes(0)
         b_transposes(1)
         w_transposes("b")
@@ -245,7 +249,8 @@ def tile_quarotfp16linear_t_kernel(tc, quantized_x, scales_x, weight, weight_sca
                 a_transposes(n, 0)
             if (n >= 1 and j == 1) or k == 2:
                 a_transposes(n, 1)
-            spread_scales(k + 3)
+            if k % 2 == 0:
+                spread_scales(k // 2 + 2)
             if k == 1:
                 w_quantise("b")
             if k == 2:

@@ -7,14 +7,17 @@ F32 = mybir.dt.float32
 U32 = mybir.dt.uint32
 U8 = mybir.dt.uint8
 ALU = mybir.AluOpType
+ACT = mybir.ActivationFunctionType
 
 P = 128
 TOKENS = 8192
 FEATURES = 1024
 OUTS = 128
 TILES = TOKENS // P
-PERIODS = TILES // 8
-PAIRS = 3 * PERIODS
+PERIOD_TILES = 16
+PERIOD_PAIRS = 7
+PERIODS = TILES // PERIOD_TILES
+PAIRS = PERIOD_PAIRS * PERIODS
 K_PASS = 512
 PASSES = FEATURES // K_PASS
 WORDS = K_PASS // 2
@@ -45,7 +48,7 @@ def tile_quarotfp16linear_t_kernel(tc, quantized_x, scales_x, weight, weight_sca
         nc.scalar.dma_start(out=ws_sb[:], in_=weight_scales)
         x_bf = {}
         x_words = {}
-        chunks = [[0, 1], [2, 3], [6, 7], [4, 5], [8, 9], [14, 15], [10, 11], [12, 13]]
+        chunks = [[0, 1], [2, 3], [4, 5], [14, 15], [6, 7], [8, 9], [10, 11], [12, 13]]
         chunks = chunks + [[t, t + 1, t + 2, t + 3] for t in range(16, TILES, 4)]
         for c, tiles in enumerate(chunks):
             n = len(tiles)
@@ -68,7 +71,10 @@ def tile_quarotfp16linear_t_kernel(tc, quantized_x, scales_x, weight, weight_sca
         nc.vector.tensor_copy(out=s32[:], in_=s_sb[:])
 
         def first_tile(k):
-            return 8 * (k // 3) + 2 * (k % 3)
+            return PERIOD_TILES * (k // PERIOD_PAIRS) + 2 * (k % PERIOD_PAIRS)
+
+        def a_tile(n, a):
+            return PERIOD_TILES * n + 2 * PERIOD_PAIRS + a
 
         s2_of = {}
 
@@ -168,6 +174,8 @@ def tile_quarotfp16linear_t_kernel(tc, quantized_x, scales_x, weight, weight_sca
             )
 
         accs = {}
+        filled = {}
+        sent = {}
 
         def multiply(tile, codes, scl, col0, step, way):
             if tile // 4 not in accs:
@@ -186,6 +194,7 @@ def tile_quarotfp16linear_t_kernel(tc, quantized_x, scales_x, weight, weight_sca
                     start=(g == 0),
                     stop=(g == PASSES - 1),
                 )
+            filled[tile // 4] = filled.get(tile // 4, 0) + 1
 
         def b_finish(k):
             codes = work.tile([P, PASSES * 2 * P], U32, align_bytes=64)
@@ -200,9 +209,9 @@ def tile_quarotfp16linear_t_kernel(tc, quantized_x, scales_x, weight, weight_sca
         def a_scale(n, a):
             if n >= PERIODS:
                 return
-            t = 8 * n + 6 + a
+            t = a_tile(n, a)
             xs = awork.tile([P, FEATURES], BF16, name="xs%d" % a)
-            nc.vector.tensor_scalar_mul(out=xs[:], in0=x_bf[t], scalar1=s32[:, t : t + 1])
+            nc.scalar.activation(out=xs[:], in_=x_bf[t], func=ACT.Copy, scale=s32[:, t : t + 1])
             xs_of[(n, a)] = xs
 
         def a_transposes(n, a):
@@ -221,12 +230,15 @@ def tile_quarotfp16linear_t_kernel(tc, quantized_x, scales_x, weight, weight_sca
                 out=codes_a[:].bitcast(FP8X4), scales=scl_a[:], in_=ga_of[n][:].rearrange("p a g r t -> p (a g r t)")
             )
             for a in range(2):
-                multiply(8 * n + 6 + a, codes_a, scl_a, a * PASSES * P, P, "a")
+                multiply(a_tile(n, a), codes_a, scl_a, a * PASSES * P, P, "a")
 
-        def send(bank):
-            result = res.tile([P, 4, OUTS], F32)
-            nc.scalar.copy(out=result[:].rearrange("p t o -> p (t o)"), in_=accs[bank][:])
-            nc.sync.dma_start(out=out_view[:, 4 * bank : 4 * bank + 4, :], in_=result[:])
+        def send_ready():
+            for bank in sorted(filled):
+                if filled[bank] == 4 and bank not in sent:
+                    result = res.tile([P, 4, OUTS], F32)
+                    nc.scalar.copy(out=result[:].rearrange("p t o -> p (t o)"), in_=accs[bank][:])
+                    nc.sync.dma_start(out=out_view[:, 4 * bank : 4 * bank + 4, :], in_=result[:])
+                    sent[bank] = True
 
         spread_scales(0)
         spread_scales(1)
@@ -235,19 +247,16 @@ def tile_quarotfp16linear_t_kernel(tc, quantized_x, scales_x, weight, weight_sca
         w_transposes("b")
         b_transposes(2)
         for k in range(PAIRS):
-            n, j = k // 3, k % 3
+            n, j = k // PERIOD_PAIRS, k % PERIOD_PAIRS
             b_scale(k, 0)
             b_transposes(2 * k + 3)
             b_scale(k, 1)
             b_transposes(2 * k + 4)
             if k == 0:
                 w_transposes("a")
-            if k == 1:
-                a_scale(0, 0)
-                a_scale(0, 1)
-            if (n >= 1 and j == 0) or k == 1:
+            if j == 3:
                 a_transposes(n, 0)
-            if (n >= 1 and j == 1) or k == 2:
+            if j == 4:
                 a_transposes(n, 1)
             if k % 2 == 0:
                 spread_scales(k // 2 + 2)
@@ -259,13 +268,10 @@ def tile_quarotfp16linear_t_kernel(tc, quantized_x, scales_x, weight, weight_sca
                 b_finish(k - 1)
             if j == 0 and n >= 1:
                 a_finish(n - 1)
-            if j == 2:
-                a_scale(n + 1, 0)
-                a_scale(n + 1, 1)
-            if j == 2:
-                send(2 * n)
-            if j == 0 and n >= 1:
-                send(2 * n - 1)
+            send_ready()
+            if j == 1:
+                a_scale(n, 0)
+                a_scale(n, 1)
         a_finish(PERIODS - 1)
         b_finish(PAIRS - 1)
-        send(2 * PERIODS - 1)
+        send_ready()

@@ -131,10 +131,17 @@ def tile_quarotfp16linear_t_kernel(tc, quantized_x, scales_x, weight, weight_sca
             w_grouped[way] = wg
 
         def w_quantise(way):
-            wc = keep.tile([P, PASSES * OUTS], U32, name="wc_" + way, align_bytes=64)
-            wsc = keep.tile([P, PASSES * OUTS], U8, name="wsc_" + way, align_bytes=64)
+            wc = keep.tile([P, (PASSES + 1) * OUTS], U32, name="wc_" + way, align_bytes=64)
+            wsc = keep.tile([P, (PASSES + 1) * OUTS], U8, name="wsc_" + way, align_bytes=64)
             nc.vector.quantize_mx(
-                out=wc[:].bitcast(FP8X4), scales=wsc[:], in_=w_grouped[way][:].rearrange("p g o t -> p (g o t)")
+                out=wc[:, 0 : PASSES * OUTS].bitcast(FP8X4),
+                scales=wsc[:, 0 : PASSES * OUTS],
+                in_=w_grouped[way][:].rearrange("p g o t -> p (g o t)"),
+            )
+            nc.vector.quantize_mx(
+                out=wc[:, PASSES * OUTS :].bitcast(FP8X4),
+                scales=wsc[:, PASSES * OUTS :],
+                in_=w_grouped[way][:, 0, :, :].rearrange("p o t -> p (o t)"),
             )
             w_codes[way] = wc
             w_scl[way] = wsc
@@ -182,11 +189,12 @@ def tile_quarotfp16linear_t_kernel(tc, quantized_x, scales_x, weight, weight_sca
                 acc = acc_pool.tile([P, 4 * OUTS], F32)
                 accs[tile // 4] = acc
             slot = tile % 4
+            width = 2 * OUTS if slot % 2 == 0 else OUTS
             for g in range(PASSES):
                 cols = slice(col0 + g * step, col0 + g * step + P)
-                w_c = slice(g * OUTS, (g + 1) * OUTS)
+                w_c = slice(g * OUTS, g * OUTS + width)
                 nc.tensor.matmul_mx(
-                    out=accs[tile // 4][:, slot * OUTS : (slot + 1) * OUTS],
+                    out=accs[tile // 4][:, slot * OUTS : slot * OUTS + width],
                     lhsT=codes[:, cols].bitcast(FP8X4),
                     lhsT_scale=scl[:, cols],
                     rhs=w_codes[way][:, w_c].bitcast(FP8X4),

@@ -7,20 +7,16 @@ F32 = mybir.dt.float32
 U32 = mybir.dt.uint32
 U8 = mybir.dt.uint8
 ALU = mybir.AluOpType
-ACT = mybir.ActivationFunctionType
 
 P = 128
 TOKENS = 8192
 FEATURES = 1024
 OUTS = 128
 TILES = TOKENS // P
-PERIOD_TILES = 16
-PERIOD_PAIRS = 7
-PERIODS = TILES // PERIOD_TILES
-PAIRS = PERIOD_PAIRS * PERIODS
+PAIRS = TILES // 2
 K_PASS = 512
 PASSES = FEATURES // K_PASS
-WORDS = K_PASS // 2
+WORDS = FEATURES // 2
 GROUPS = 8
 FLOPS = 2 * TOKENS * FEATURES * OUTS
 
@@ -31,255 +27,140 @@ def tile_quarotfp16linear_t_kernel(tc, quantized_x, scales_x, weight, weight_sca
     s_view = scales_x.flatten_outer_dims().rearrange("(p t) o -> p (t o)", t=TILES)
     out_view = out.flatten_outer_dims().rearrange("(p t) o -> p t o", t=TILES)
 
-    with tc.tile_pool(name="keep", bufs=1) as keep, tc.tile_pool(name="spread", bufs=4) as spread, tc.tile_pool(
-        name="work", bufs=3
-    ) as work, tc.tile_pool(name="awork", bufs=2) as awork, tc.tile_pool(name="res", bufs=16) as res, tc.psum_pool(
-        name="xb", bufs=3
-    ) as xb_pool, tc.psum_pool(name="aux", bufs=3) as aux_pool, tc.psum_pool(
+    with tc.tile_pool(name="keep", bufs=1) as keep, tc.tile_pool(name="scaled", bufs=6) as scaled, tc.tile_pool(
+        name="work", bufs=4
+    ) as work, tc.tile_pool(name="res", bufs=16) as res, tc.psum_pool(name="xb", bufs=6) as xb_pool, tc.psum_pool(
         name="acc", bufs=2
     ) as acc_pool, tc.manual_schedule():
         s_sb = keep.tile([P, TILES], BF16)
-        nc.sync.dma_start(out=s_sb[:], in_=s_view)
-        w_sb = keep.tile([P, FEATURES], BF16)
-        nc.scalar.dma_start(out=w_sb[:], in_=weight)
+        nc.scalar.dma_start(out=s_sb[:], in_=s_view)
         off_sb = keep.tile([P, GROUPS], BF16)
         nc.scalar.dma_start(out=off_sb[:], in_=offset_w)
         ws_sb = keep.tile([P, GROUPS], BF16)
         nc.scalar.dma_start(out=ws_sb[:], in_=weight_scales)
         x_bf = {}
-        x_words = {}
-        chunks = [[0, 1], [2, 3], [4, 5], [14, 15], [6, 7], [8, 9], [10, 11], [12, 13]]
-        chunks = chunks + [[t, t + 1, t + 2, t + 3] for t in range(16, TILES, 4)]
+        chunks = [[0], [1], [2, 3], [4, 5], [6, 7]] + [[t, t + 1, t + 2, t + 3] for t in range(8, TILES, 4)]
+        w_sb = keep.tile([P, FEATURES], BF16)
         for c, tiles in enumerate(chunks):
             n = len(tiles)
             xc = keep.tile([P, n, FEATURES], BF16, name="xc%d" % c)
             nc.sync.dma_start(out=xc[:], in_=x_view[:, tiles[0] : tiles[0] + n, :])
-            words = xc[:].rearrange("p n k -> p (n k)").bitcast(F32)
             for i, t in enumerate(tiles):
                 x_bf[t] = xc[:, i, :]
-                x_words[t] = words[:, i * (FEATURES // 2) : (i + 1) * (FEATURES // 2)]
+            if c == 1:
+                nc.sync.dma_start(out=w_sb[:], in_=weight)
 
-        ident_f32 = keep.tile([P, P], F32)
-        make_identity(nc, ident_f32[:])
-        ident_bf = keep.tile([P, P], BF16)
-        make_identity(nc, ident_bf[:])
-
-        s_pair = keep.tile([P, TILES, 2], BF16)
-        nc.vector.tensor_copy(out=s_pair[:], in_=s_sb[:].unsqueeze(2).to_broadcast([P, TILES, 2]))
-        s_words = s_pair[:].rearrange("p t e -> p (t e)").bitcast(F32)
-        s32 = keep.tile([P, TILES], F32)
-        nc.vector.tensor_copy(out=s32[:], in_=s_sb[:])
-
-        def first_tile(k):
-            return PERIOD_TILES * (k // PERIOD_PAIRS) + 2 * (k % PERIOD_PAIRS)
-
-        def a_tile(n, a):
-            return PERIOD_TILES * n + 2 * PERIOD_PAIRS + a
-
-        s2_of = {}
-
-        def spread_scales(q):
-            if 2 * q >= PAIRS:
-                return
-            bank = aux_pool.tile([P, 4, P], F32, tag="aux")
-            for i in range(4):
-                t = first_tile(2 * q + i // 2) + i % 2
-                nc.tensor.transpose(out=bank[:, i, :], in_=s_words[:, t : t + 1].to_broadcast([P, P]), identity=ident_f32[:])
-            s2 = spread.tile([P, 4 * P], F32)
-            nc.scalar.copy(out=s2[:], in_=bank[:].rearrange("p i r -> p (i r)"))
-            s2_of[q] = s2
-
-        off32 = keep.tile([P, GROUPS], F32)
-        nc.vector.tensor_copy(out=off32[:], in_=off_sb[:])
-        ws32 = keep.tile([P, GROUPS], F32)
-        nc.vector.tensor_copy(out=ws32[:], in_=ws_sb[:])
-        noff32 = keep.tile([P, GROUPS], F32)
-        nc.vector.tensor_scalar(out=noff32[:], in0=off_sb[:], scalar1=-1.0, scalar2=None, op0=ALU.mult)
-        w_deq_b = keep.tile([P, PASSES, 2, 2, P], BF16)
-        for q in range(GROUPS):
-            g, u, h = q // 4, (q // 2) % 2, q % 2
-            nc.vector.tensor_scalar(
-                out=w_deq_b[:, g, u, :, 64 * h : 64 * h + 64],
-                in0=w_sb[:, q * P : (q + 1) * P].rearrange("p (m e) -> p e m", e=2),
-                scalar1=off32[:, q : q + 1],
-                scalar2=ws32[:, q : q + 1],
-                op0=ALU.subtract,
-                op1=ALU.mult,
-            )
-        w_deq_a = keep.tile([P, FEATURES], BF16)
-        for q in range(GROUPS):
-            nc.gpsimd.tensor_scalar(
-                out=w_deq_a[:, q * P : (q + 1) * P],
-                in0=w_sb[:, q * P : (q + 1) * P],
-                scalar1=noff32[:, q : q + 1],
-                scalar2=ws32[:, q : q + 1],
-                op0=ALU.add,
-                op1=ALU.mult,
-            )
-        w_grouped = {}
-        w_codes = {}
-        w_scl = {}
-
-        def w_transposes(way):
-            wt = aux_pool.tile([P, PASSES * 4, OUTS], BF16, tag="aux")
-            for g in range(PASSES):
-                for t in range(4):
-                    src = w_deq_b[:, g, t // 2, t % 2, :] if way == "b" else w_deq_a[:, g * K_PASS + t * P : g * K_PASS + (t + 1) * P]
-                    nc.tensor.transpose(out=wt[:, g * 4 + t, :], in_=src, identity=ident_bf[:])
-            wg = keep.tile([P, PASSES, OUTS, 4], BF16, name="wg_" + way, align_bytes=64)
-            nc.scalar.copy(out=wg[:], in_=wt[:].rearrange("p (g t) o -> p g o t", g=PASSES))
-            w_grouped[way] = wg
-
-        def w_quantise(way):
-            wc = keep.tile([P, (PASSES + 1) * OUTS], U32, name="wc_" + way, align_bytes=64)
-            wsc = keep.tile([P, (PASSES + 1) * OUTS], U8, name="wsc_" + way, align_bytes=64)
-            nc.vector.quantize_mx(
-                out=wc[:, 0 : PASSES * OUTS].bitcast(FP8X4),
-                scales=wsc[:, 0 : PASSES * OUTS],
-                in_=w_grouped[way][:].rearrange("p g o t -> p (g o t)"),
-            )
-            nc.vector.quantize_mx(
-                out=wc[:, PASSES * OUTS :].bitcast(FP8X4),
-                scales=wsc[:, PASSES * OUTS :],
-                in_=w_grouped[way][:, 0, :, :].rearrange("p o t -> p (o t)"),
-            )
-            w_codes[way] = wc
-            w_scl[way] = wsc
-
-        banks = {}
-
-        def b_transposes(i):
-            k, g = i // 2, i % 2
-            if k >= PAIRS:
-                return
-            bank = xb_pool.tile([P, 2, 2 * P], F32, tag="xb")
-            for j in range(2):
-                for u in range(2):
-                    lo = g * WORDS + u * P
-                    nc.tensor.transpose(
-                        out=bank[:, u, j * P : (j + 1) * P],
-                        in_=x_words[first_tile(k) + j][:, lo : lo + P],
-                        identity=ident_f32[:],
-                    )
-            banks[i] = bank
-
-        grouped_of = {}
-
-        def b_scale(k, g):
-            if g == 0:
-                grouped = work.tile([P, PASSES, 2 * P * 4], BF16, align_bytes=64)
-                grouped_of[k] = grouped
-            nc.vector.tensor_tensor(
-                out=grouped_of[k][:, g, :].rearrange("p (c u e) -> p c u e", u=2, e=2),
-                in0=banks[2 * k + g][:].rearrange("p u c -> p (u c)").bitcast(BF16).rearrange("p (u c e) -> p c u e", u=2, e=2),
-                in1=s2_of[k // 2][:, (k % 2) * 2 * P : (k % 2 + 1) * 2 * P]
-                .bitcast(BF16)
-                .rearrange("p (c e) -> p c e", e=2)
-                .unsqueeze(2)
-                .to_broadcast([P, 2 * P, 2, 2]),
-                op=ALU.mult,
-            )
-
-        accs = {}
-        filled = {}
-        sent = {}
-
-        def multiply(tile, codes, scl, col0, step, way):
-            if tile // 4 not in accs:
-                acc = acc_pool.tile([P, 4 * OUTS], F32)
-                accs[tile // 4] = acc
-            slot = tile % 4
-            width = 2 * OUTS if slot % 2 == 0 else OUTS
-            for g in range(PASSES):
-                cols = slice(col0 + g * step, col0 + g * step + P)
-                w_c = slice(g * OUTS, g * OUTS + width)
-                nc.tensor.matmul_mx(
-                    out=accs[tile // 4][:, slot * OUTS : slot * OUTS + width],
-                    lhsT=codes[:, cols].bitcast(FP8X4),
-                    lhsT_scale=scl[:, cols],
-                    rhs=w_codes[way][:, w_c].bitcast(FP8X4),
-                    rhs_scale=w_scl[way][:, w_c],
-                    start=(g == 0),
-                    stop=(g == PASSES - 1),
-                )
-            filled[tile // 4] = filled.get(tile // 4, 0) + 1
-
-        def b_finish(k):
-            codes = work.tile([P, PASSES * 2 * P], U32, align_bytes=64)
-            scl = work.tile([P, PASSES * 2 * P], U8, align_bytes=64)
-            nc.vector.quantize_mx(out=codes[:].bitcast(FP8X4), scales=scl[:], in_=grouped_of[k][:].rearrange("p g c -> p (g c)"))
-            for j in range(2):
-                multiply(first_tile(k) + j, codes, scl, j * P, 2 * P, "b")
+        ident = keep.tile([P, P], F32)
+        make_identity(nc, ident[:])
 
         xs_of = {}
-        ga_of = {}
+        bank_of = {}
+        grouped_of = {}
+        codes_of = {}
 
-        def a_scale(n, a):
-            if n >= PERIODS:
-                return
-            t = a_tile(n, a)
-            xs = awork.tile([P, FEATURES], BF16, name="xs%d" % a)
-            nc.scalar.activation(out=xs[:], in_=x_bf[t], func=ACT.Copy, scale=s32[:, t : t + 1])
-            xs_of[(n, a)] = xs
+        def scale(t):
+            xs = scaled.tile([P, FEATURES], BF16)
+            nc.vector.tensor_scalar(out=xs[:], in0=x_bf[t], scalar1=s_sb[:, t : t + 1], scalar2=None, op0=ALU.mult)
+            xs_of[t] = xs
 
-        def a_transposes(n, a):
-            bank = aux_pool.tile([P, PASSES * 4, P], BF16, tag="aux")
-            for i in range(PASSES * 4):
-                nc.tensor.transpose(out=bank[:, i, :], in_=xs_of[(n, a)][:, i * P : (i + 1) * P], identity=ident_bf[:])
-            if a == 0:
-                ga = awork.tile([P, 2, PASSES, P, 4], BF16, align_bytes=64)
-                ga_of[n] = ga
-            nc.scalar.copy(out=ga_of[n][:, a, :, :, :], in_=bank[:].rearrange("p (g t) r -> p g r t", g=PASSES))
+        def transposes(key, src):
+            bank = xb_pool.tile([P, PASSES * 2, P], F32, tag="xb")
+            words = src[:].bitcast(F32)
+            for i in range(PASSES * 2):
+                nc.tensor.transpose(out=bank[:, i, :], in_=words[:, i * P : (i + 1) * P], identity=ident[:])
+            bank_of[key] = bank
 
-        def a_finish(n):
-            codes_a = awork.tile([P, 2 * PASSES * P], U32, align_bytes=64)
-            scl_a = awork.tile([P, 2 * PASSES * P], U8, align_bytes=64)
-            nc.vector.quantize_mx(
-                out=codes_a[:].bitcast(FP8X4), scales=scl_a[:], in_=ga_of[n][:].rearrange("p a g r t -> p (a g r t)")
-            )
+        def regroup(key, dst, on_vector):
+            o = dst.rearrange("p (g r u) -> p g r u", g=PASSES, u=2)
+            i = bank_of[key][:].rearrange("p (g u) r -> p g r u", g=PASSES)
+            if on_vector:
+                nc.vector.tensor_copy(out=o, in_=i)
+            else:
+                nc.scalar.copy(out=o, in_=i)
+
+        def regroup_pair(j):
+            grouped = work.tile([P, 2 * FEATURES], BF16, align_bytes=64)
+            words = grouped[:].bitcast(F32)
             for a in range(2):
-                multiply(a_tile(n, a), codes_a, scl_a, a * PASSES * P, P, "a")
+                t = 2 * j + a
+                regroup(t, words[:, a * WORDS : (a + 1) * WORDS], t % 16 == 9)
+            grouped_of[j] = grouped
 
-        def send_ready():
-            for bank in sorted(filled):
-                if filled[bank] == 4 and bank not in sent:
-                    result = res.tile([P, 4, OUTS], F32)
-                    nc.scalar.copy(out=result[:].rearrange("p t o -> p (t o)"), in_=accs[bank][:])
-                    nc.sync.dma_start(out=out_view[:, 4 * bank : 4 * bank + 4, :], in_=result[:])
-                    sent[bank] = True
+        def quantise_pair(j):
+            codes = work.tile([P, 2 * PASSES * P], U32, align_bytes=64)
+            scl = work.tile([P, 2 * PASSES * P], U8, align_bytes=64)
+            nc.vector.quantize_mx(out=codes[:].bitcast(FP8X4), scales=scl[:], in_=grouped_of[j][:])
+            codes_of[j] = (codes, scl)
 
-        spread_scales(0)
-        spread_scales(1)
-        b_transposes(0)
-        b_transposes(1)
-        w_transposes("b")
-        b_transposes(2)
-        for k in range(PAIRS):
-            n, j = k // PERIOD_PAIRS, k % PERIOD_PAIRS
-            b_scale(k, 0)
-            b_transposes(2 * k + 3)
-            b_scale(k, 1)
-            b_transposes(2 * k + 4)
-            if k == 0:
-                w_transposes("a")
-            if j == 3:
-                a_transposes(n, 0)
-            if j == 4:
-                a_transposes(n, 1)
-            if k % 2 == 0:
-                spread_scales(k // 2 + 2)
-            if k == 1:
-                w_quantise("b")
-            if k == 2:
-                w_quantise("a")
-            if k >= 1:
-                b_finish(k - 1)
-            if j == 0 and n >= 1:
-                a_finish(n - 1)
-            send_ready()
-            if j == 1:
-                a_scale(n, 0)
-                a_scale(n, 1)
-        a_finish(PERIODS - 1)
-        b_finish(PAIRS - 1)
-        send_ready()
+        w_deq = keep.tile([P, FEATURES], BF16)
+        w_grouped = keep.tile([P, FEATURES], BF16, align_bytes=64)
+        wc = keep.tile([P, (PASSES + 1) * OUTS], U32, align_bytes=64)
+        wsc = keep.tile([P, (PASSES + 1) * OUTS], U8, align_bytes=64)
+
+        def w_dequantise():
+            for q in range(GROUPS):
+                nc.vector.tensor_scalar(
+                    out=w_deq[:, q * P : (q + 1) * P],
+                    in0=w_sb[:, q * P : (q + 1) * P],
+                    scalar1=off_sb[:, q : q + 1],
+                    scalar2=ws_sb[:, q : q + 1],
+                    op0=ALU.subtract,
+                    op1=ALU.mult,
+                )
+
+        def w_quantise():
+            n = PASSES * OUTS
+            nc.vector.quantize_mx(out=wc[:, 0:n].bitcast(FP8X4), scales=wsc[:, 0:n], in_=w_grouped[:])
+            nc.vector.quantize_mx(out=wc[:, n:].bitcast(FP8X4), scales=wsc[:, n:], in_=w_grouped[:, 0 : 4 * OUTS])
+
+        acc_of = {}
+
+        def multiply_pair(j):
+            codes, scl = codes_of[j]
+            for a in range(2):
+                t = 2 * j + a
+                if t % 4 == 0:
+                    acc = acc_pool.tile([P, 4 * OUTS], F32)
+                    acc_of[t // 4] = acc
+                slot = t % 4
+                width = 2 * OUTS if a == 0 else OUTS
+                for g in range(PASSES):
+                    cols = slice((a * PASSES + g) * P, (a * PASSES + g + 1) * P)
+                    w_cols = slice(g * OUTS, g * OUTS + width)
+                    nc.tensor.matmul_mx(
+                        out=acc_of[t // 4][:, slot * OUTS : slot * OUTS + width],
+                        lhsT=codes[:, cols].bitcast(FP8X4),
+                        lhsT_scale=scl[:, cols],
+                        rhs=wc[:, w_cols].bitcast(FP8X4),
+                        rhs_scale=wsc[:, w_cols],
+                        start=(g == 0),
+                        stop=(g == PASSES - 1),
+                    )
+
+        def send(b):
+            result = res.tile([P, 4, OUTS], F32)
+            nc.scalar.copy(out=result[:].rearrange("p t o -> p (t o)"), in_=acc_of[b][:])
+            nc.sync.dma_start(out=out_view[:, 4 * b : 4 * b + 4, :], in_=result[:])
+
+        scale(0)
+        scale(1)
+        for i in range(PAIRS + 2):
+            if i + 1 < PAIRS:
+                scale(2 * i + 2)
+                scale(2 * i + 3)
+            if i < PAIRS:
+                transposes(2 * i, xs_of[2 * i])
+                transposes(2 * i + 1, xs_of[2 * i + 1])
+                regroup_pair(i)
+            if i == 0:
+                w_dequantise()
+                transposes("w", w_deq)
+                regroup("w", w_grouped[:].bitcast(F32), False)
+            if i == 1:
+                w_quantise()
+            if 1 <= i <= PAIRS:
+                quantise_pair(i - 1)
+            if i >= 2:
+                multiply_pair(i - 2)
+                if (i - 2) % 2 == 1:
+                    send((i - 2) // 2)

@@ -94,8 +94,8 @@ def tile_quarotfp16linear_t_kernel(tc, quantized_x, scales_x, weight, weight_sca
 
         w_deq = keep.tile([P, FEATURES], BF16)
         w_grouped = keep.tile([P, FEATURES], BF16, align_bytes=64)
-        wc = keep.tile([P, (PASSES + 1) * OUTS], U32, align_bytes=64)
-        wsc = keep.tile([P, (PASSES + 1) * OUTS], U8, align_bytes=64)
+        wc = keep.tile([P, PASSES * OUTS], U32, align_bytes=64)
+        wsc = keep.tile([P, PASSES * OUTS], U8, align_bytes=64)
 
         def w_dequantise():
             for q in range(GROUPS):
@@ -109,9 +109,7 @@ def tile_quarotfp16linear_t_kernel(tc, quantized_x, scales_x, weight, weight_sca
                 )
 
         def w_quantise():
-            n = PASSES * OUTS
-            nc.vector.quantize_mx(out=wc[:, 0:n].bitcast(FP8X4), scales=wsc[:, 0:n], in_=w_grouped[:])
-            nc.vector.quantize_mx(out=wc[:, n:].bitcast(FP8X4), scales=wsc[:, n:], in_=w_grouped[:, 0 : 4 * OUTS])
+            nc.vector.quantize_mx(out=wc[:].bitcast(FP8X4), scales=wsc[:], in_=w_grouped[:])
 
         acc_of = {}
 
@@ -123,12 +121,11 @@ def tile_quarotfp16linear_t_kernel(tc, quantized_x, scales_x, weight, weight_sca
                     acc = acc_pool.tile([P, 4 * OUTS], F32)
                     acc_of[t // 4] = acc
                 slot = t % 4
-                width = 2 * OUTS if a == 0 else OUTS
                 for g in range(PASSES):
                     cols = slice((a * PASSES + g) * P, (a * PASSES + g + 1) * P)
-                    w_cols = slice(g * OUTS, g * OUTS + width)
+                    w_cols = slice(g * OUTS, (g + 1) * OUTS)
                     nc.tensor.matmul_mx(
-                        out=acc_of[t // 4][:, slot * OUTS : slot * OUTS + width],
+                        out=acc_of[t // 4][:, slot * OUTS : (slot + 1) * OUTS],
                         lhsT=codes[:, cols].bitcast(FP8X4),
                         lhsT_scale=scl[:, cols],
                         rhs=wc[:, w_cols].bitcast(FP8X4),

@@ -27,8 +27,8 @@ def tile_quarotfp16linear_t_kernel(tc, quantized_x, scales_x, weight, weight_sca
     s_view = scales_x.flatten_outer_dims().rearrange("(p t) o -> p (t o)", t=TILES)
     out_view = out.flatten_outer_dims().rearrange("(p t) o -> p t o", t=TILES)
 
-    with tc.tile_pool(name="keep", bufs=1) as keep, tc.tile_pool(name="scaled", bufs=6) as scaled, tc.tile_pool(
-        name="work", bufs=4
+    with tc.tile_pool(name="keep", bufs=1) as keep, tc.tile_pool(name="scaled", bufs=8) as scaled, tc.tile_pool(
+        name="work", bufs=5
     ) as work, tc.tile_pool(name="res", bufs=16) as res, tc.psum_pool(name="xb", bufs=6) as xb_pool, tc.psum_pool(
         name="acc", bufs=2
     ) as acc_pool, tc.manual_schedule():
@@ -39,7 +39,8 @@ def tile_quarotfp16linear_t_kernel(tc, quantized_x, scales_x, weight, weight_sca
         ws_sb = keep.tile([P, GROUPS], BF16)
         nc.scalar.dma_start(out=ws_sb[:], in_=weight_scales)
         x_bf = {}
-        chunks = [[0], [1], [2, 3], [4, 5], [6, 7]] + [[t, t + 1, t + 2, t + 3] for t in range(8, TILES, 4)]
+        chunks = [[0], [1], [2], [3], [4, 5], [6, 7], [8, 9], [10, 11], [12, 13], [14, 15]]
+        chunks = chunks + [[t, t + 1, t + 2, t + 3] for t in range(16, TILES, 4)]
         w_sb = keep.tile([P, FEATURES], BF16)
         for c, tiles in enumerate(chunks):
             n = len(tiles)
@@ -47,7 +48,7 @@ def tile_quarotfp16linear_t_kernel(tc, quantized_x, scales_x, weight, weight_sca
             nc.sync.dma_start(out=xc[:], in_=x_view[:, tiles[0] : tiles[0] + n, :])
             for i, t in enumerate(tiles):
                 x_bf[t] = xc[:, i, :]
-            if c == 1:
+            if c == 4:
                 nc.sync.dma_start(out=w_sb[:], in_=weight)
 
         ident = keep.tile([P, P], F32)
@@ -83,7 +84,7 @@ def tile_quarotfp16linear_t_kernel(tc, quantized_x, scales_x, weight, weight_sca
             words = grouped[:].bitcast(F32)
             for a in range(2):
                 t = 2 * j + a
-                regroup(t, words[:, a * WORDS : (a + 1) * WORDS], t % 16 == 9)
+                regroup(t, words[:, a * WORDS : (a + 1) * WORDS], t % 8 == 5)
             grouped_of[j] = grouped
 
         def quantise_pair(j):
@@ -139,25 +140,26 @@ def tile_quarotfp16linear_t_kernel(tc, quantized_x, scales_x, weight, weight_sca
             nc.scalar.copy(out=result[:].rearrange("p t o -> p (t o)"), in_=acc_of[b][:])
             nc.sync.dma_start(out=out_view[:, 4 * b : 4 * b + 4, :], in_=result[:])
 
-        scale(0)
-        scale(1)
-        for i in range(PAIRS + 2):
-            if i + 1 < PAIRS:
-                scale(2 * i + 2)
-                scale(2 * i + 3)
+        for t in range(4):
+            scale(t)
+        for i in range(PAIRS + 4):
+            if i == 1:
+                w_dequantise()
+            if i == 3:
+                w_quantise()
+            if 2 <= i < PAIRS + 2:
+                quantise_pair(i - 2)
+            if i + 2 < PAIRS:
+                scale(2 * i + 4)
+                scale(2 * i + 5)
             if i < PAIRS:
                 transposes(2 * i, xs_of[2 * i])
                 transposes(2 * i + 1, xs_of[2 * i + 1])
                 regroup_pair(i)
-            if i == 0:
-                w_dequantise()
+            if i == 2:
                 transposes("w", w_deq)
                 regroup("w", w_grouped[:].bitcast(F32), False)
-            if i == 1:
-                w_quantise()
-            if 1 <= i <= PAIRS:
-                quantise_pair(i - 1)
-            if i >= 2:
-                multiply_pair(i - 2)
-                if (i - 2) % 2 == 1:
-                    send((i - 2) // 2)
+            if i >= 4:
+                multiply_pair(i - 4)
+                if (i - 4) % 2 == 1:
+                    send((i - 4) // 2)

@@ -27,9 +27,9 @@ def tile_quarotfp16linear_t_kernel(tc, quantized_x, scales_x, weight, weight_sca
     s_view = scales_x.flatten_outer_dims().rearrange("(p t) o -> p (t o)", t=TILES)
     out_view = out.flatten_outer_dims().rearrange("(p t) o -> p t o", t=TILES)
 
-    with tc.tile_pool(name="keep", bufs=1) as keep, tc.tile_pool(name="scaled", bufs=8) as scaled, tc.tile_pool(
-        name="work", bufs=5
-    ) as work, tc.tile_pool(name="res", bufs=16) as res, tc.psum_pool(name="xb", bufs=6) as xb_pool, tc.psum_pool(
+    with tc.tile_pool(name="keep", bufs=1) as keep, tc.tile_pool(
+        name="work", bufs=6
+    ) as work, tc.psum_pool(name="xb", bufs=6) as xb_pool, tc.psum_pool(
         name="acc", bufs=2
     ) as acc_pool, tc.manual_schedule():
         s_sb = keep.tile([P, TILES], BF16)
@@ -54,19 +54,16 @@ def tile_quarotfp16linear_t_kernel(tc, quantized_x, scales_x, weight, weight_sca
         ident = keep.tile([P, P], F32)
         make_identity(nc, ident[:])
 
-        xs_of = {}
         bank_of = {}
         grouped_of = {}
         codes_of = {}
 
         def scale(t):
-            xs = scaled.tile([P, FEATURES], BF16)
-            nc.vector.tensor_scalar(out=xs[:], in0=x_bf[t], scalar1=s_sb[:, t : t + 1], scalar2=None, op0=ALU.mult)
-            xs_of[t] = xs
+            nc.vector.tensor_scalar(out=x_bf[t], in0=x_bf[t], scalar1=s_sb[:, t : t + 1], scalar2=None, op0=ALU.mult)
 
         def transposes(key, src):
             bank = xb_pool.tile([P, PASSES * 2, P], F32, tag="xb")
-            words = src[:].bitcast(F32)
+            words = src.bitcast(F32)
             for i in range(PASSES * 2):
                 nc.tensor.transpose(out=bank[:, i, :], in_=words[:, i * P : (i + 1) * P], identity=ident[:])
             bank_of[key] = bank
@@ -87,10 +84,16 @@ def tile_quarotfp16linear_t_kernel(tc, quantized_x, scales_x, weight, weight_sca
                 regroup(t, words[:, a * WORDS : (a + 1) * WORDS], t % 8 == 5)
             grouped_of[j] = grouped
 
-        def quantise_pair(j):
+        def quantise_pair(j, parts):
             codes = work.tile([P, 2 * PASSES * P], U32, align_bytes=64)
             scl = work.tile([P, 2 * PASSES * P], U8, align_bytes=64)
-            nc.vector.quantize_mx(out=codes[:].bitcast(FP8X4), scales=scl[:], in_=grouped_of[j][:])
+            n = 2 * PASSES * P // parts
+            for a in range(parts):
+                nc.vector.quantize_mx(
+                    out=codes[:, a * n : (a + 1) * n].bitcast(FP8X4),
+                    scales=scl[:, a * n : (a + 1) * n],
+                    in_=grouped_of[j][:, 4 * a * n : 4 * (a + 1) * n],
+                )
             codes_of[j] = (codes, scl)
 
         w_deq = keep.tile([P, FEATURES], BF16)
@@ -114,52 +117,66 @@ def tile_quarotfp16linear_t_kernel(tc, quantized_x, scales_x, weight, weight_sca
 
         acc_of = {}
 
-        def multiply_pair(j):
-            codes, scl = codes_of[j]
-            for a in range(2):
-                t = 2 * j + a
-                if t % 4 == 0:
-                    acc = acc_pool.tile([P, 4 * OUTS], F32)
-                    acc_of[t // 4] = acc
-                slot = t % 4
-                for g in range(PASSES):
-                    cols = slice((a * PASSES + g) * P, (a * PASSES + g + 1) * P)
-                    w_cols = slice(g * OUTS, (g + 1) * OUTS)
-                    nc.tensor.matmul_mx(
-                        out=acc_of[t // 4][:, slot * OUTS : (slot + 1) * OUTS],
-                        lhsT=codes[:, cols].bitcast(FP8X4),
-                        lhsT_scale=scl[:, cols],
-                        rhs=wc[:, w_cols].bitcast(FP8X4),
-                        rhs_scale=wsc[:, w_cols],
-                        start=(g == 0),
-                        stop=(g == PASSES - 1),
-                    )
+        def multiply(t):
+            codes, scl = codes_of[t // 2]
+            if t % 4 == 0 or t == TILES - 1:
+                acc = acc_pool.tile([P, 4 * OUTS], F32)
+            else:
+                acc = acc_of[t - 1]
+            acc_of[t] = acc
+            slot = t % 4
+            for g in range(PASSES):
+                cols = slice((t % 2 * PASSES + g) * P, (t % 2 * PASSES + g + 1) * P)
+                w_cols = slice(g * OUTS, (g + 1) * OUTS)
+                nc.tensor.matmul_mx(
+                    out=acc[:, slot * OUTS : (slot + 1) * OUTS],
+                    lhsT=codes[:, cols].bitcast(FP8X4),
+                    lhsT_scale=scl[:, cols],
+                    rhs=wc[:, w_cols].bitcast(FP8X4),
+                    rhs_scale=wsc[:, w_cols],
+                    start=(g == 0),
+                    stop=(g == PASSES - 1),
+                )
 
-        def send(b):
-            result = res.tile([P, 4, OUTS], F32)
-            nc.scalar.copy(out=result[:].rearrange("p t o -> p (t o)"), in_=acc_of[b][:])
-            nc.sync.dma_start(out=out_view[:, 4 * b : 4 * b + 4, :], in_=result[:])
+        results = keep.tile([P, TILES, OUTS], F32)
+        store_ends = [16, 32, 48, 56, 60, 63, 64]
 
+        def send(t0, t1):
+            slot = t0 % 4
+            nc.scalar.copy(
+                out=results[:, t0:t1, :].rearrange("p t o -> p (t o)"),
+                in_=acc_of[t0][:, slot * OUTS : (slot + t1 - t0) * OUTS],
+            )
+            if t1 in store_ends:
+                first = max([0] + [e for e in store_ends if e < t1])
+                nc.sync.dma_start(out=out_view[:, first:t1, :], in_=results[:, first:t1, :])
+
+        multiplied = 0
         for t in range(4):
             scale(t)
         for i in range(PAIRS + 4):
             if i == 1:
                 w_dequantise()
-            if i == 3:
-                w_quantise()
             if 2 <= i < PAIRS + 2:
-                quantise_pair(i - 2)
+                quantise_pair(i - 2, 2 if i - 2 == PAIRS - 1 else 1)
             if i + 2 < PAIRS:
                 scale(2 * i + 4)
                 scale(2 * i + 5)
             if i < PAIRS:
-                transposes(2 * i, xs_of[2 * i])
-                transposes(2 * i + 1, xs_of[2 * i + 1])
+                transposes(2 * i, x_bf[2 * i])
+                transposes(2 * i + 1, x_bf[2 * i + 1])
                 regroup_pair(i)
             if i == 2:
-                transposes("w", w_deq)
+                transposes("w", w_deq[:])
                 regroup("w", w_grouped[:].bitcast(F32), False)
-            if i >= 4:
-                multiply_pair(i - 4)
-                if (i - 4) % 2 == 1:
-                    send((i - 4) // 2)
+            if i == 3:
+                w_quantise()
+            while multiplied < PAIRS and multiplied <= i - (5 - (i >= 12) - (i >= 20)):
+                j = multiplied
+                for a in range(2):
+                    multiply(2 * j + a)
+                    if j == PAIRS - 1:
+                        send(*((TILES - 4, TILES - 1) if a == 0 else (TILES - 1, TILES)))
+                if j % 2 == 1 and j < PAIRS - 1:
+                    send(2 * j - 2, 2 * j + 2)
+                multiplied += 1

@@ -81,7 +81,7 @@ def tile_quarotfp16linear_t_kernel(tc, quantized_x, scales_x, weight, weight_sca
             words = grouped[:].bitcast(F32)
             for a in range(2):
                 t = 2 * j + a
-                regroup(t, words[:, a * WORDS : (a + 1) * WORDS], t % 8 == 5)
+                regroup(t, words[:, a * WORDS : (a + 1) * WORDS], t % 16 == 9)
             grouped_of[j] = grouped
 
         def quantise_pair(j, parts):

@@ -98,8 +98,8 @@ def tile_quarotfp16linear_t_kernel(tc, quantized_x, scales_x, weight, weight_sca
 
         w_deq = keep.tile([P, FEATURES], BF16)
         w_grouped = keep.tile([P, FEATURES], BF16, align_bytes=64)
-        wc = keep.tile([P, PASSES * OUTS], U32, align_bytes=64)
-        wsc = keep.tile([P, PASSES * OUTS], U8, align_bytes=64)
+        wc = keep.tile([P, (PASSES + 1) * OUTS], U32, align_bytes=64)
+        wsc = keep.tile([P, (PASSES + 1) * OUTS], U8, align_bytes=64)
 
         def w_dequantise():
             for q in range(GROUPS):
@@ -113,7 +113,9 @@ def tile_quarotfp16linear_t_kernel(tc, quantized_x, scales_x, weight, weight_sca
                 )
 
         def w_quantise():
-            nc.vector.quantize_mx(out=wc[:].bitcast(FP8X4), scales=wsc[:], in_=w_grouped[:])
+            n = PASSES * OUTS
+            nc.vector.quantize_mx(out=wc[:, 0:n].bitcast(FP8X4), scales=wsc[:, 0:n], in_=w_grouped[:])
+            nc.vector.quantize_mx(out=wc[:, n:].bitcast(FP8X4), scales=wsc[:, n:], in_=w_grouped[:, 0 : 4 * OUTS])
 
         acc_of = {}
 
@@ -125,11 +127,12 @@ def tile_quarotfp16linear_t_kernel(tc, quantized_x, scales_x, weight, weight_sca
                 acc = acc_of[t - 1]
             acc_of[t] = acc
             slot = t % 4
+            width = 2 * OUTS if t % 2 == 0 else OUTS
             for g in range(PASSES):
                 cols = slice((t % 2 * PASSES + g) * P, (t % 2 * PASSES + g + 1) * P)
-                w_cols = slice(g * OUTS, (g + 1) * OUTS)
+                w_cols = slice(g * OUTS, g * OUTS + width)
                 nc.tensor.matmul_mx(
-                    out=acc[:, slot * OUTS : (slot + 1) * OUTS],
+                    out=acc[:, slot * OUTS : slot * OUTS + width],
                     lhsT=codes[:, cols].bitcast(FP8X4),
                     lhsT_scale=scl[:, cols],
                     rhs=wc[:, w_cols].bitcast(FP8X4),

import concourse.mybir as mybir
from concourse.masks import make_identity

FP8X4 = mybir.dt.float8_e4m3fn_x4
BF16 = mybir.dt.bfloat16
F32 = mybir.dt.float32
U32 = mybir.dt.uint32
U8 = mybir.dt.uint8
ALU = mybir.AluOpType

P = 128
TOKENS = 8192
FEATURES = 1024
OUTS = 128
TILES = TOKENS // P
PAIRS = TILES // 2
K_PASS = 512
PASSES = FEATURES // K_PASS
WORDS = FEATURES // 2
GROUPS = 8
FLOPS = 2 * TOKENS * FEATURES * OUTS


def tile_quarotfp16linear_t_kernel(tc, quantized_x, scales_x, weight, weight_scales, offset_w, out):
    nc = tc.nc
    x_view = quantized_x.flatten_outer_dims().rearrange("(p t) k -> p t k", t=TILES)
    s_view = scales_x.flatten_outer_dims().rearrange("(p t) o -> p (t o)", t=TILES)
    out_view = out.flatten_outer_dims().rearrange("(p t) o -> p t o", t=TILES)

    with tc.tile_pool(name="keep", bufs=1) as keep, tc.tile_pool(
        name="work", bufs=6
    ) as work, tc.psum_pool(name="xb", bufs=6) as xb_pool, tc.psum_pool(
        name="acc", bufs=2
    ) as acc_pool, tc.manual_schedule():
        s_sb = keep.tile([P, TILES], BF16)
        nc.scalar.dma_start(out=s_sb[:], in_=s_view)
        off_sb = keep.tile([P, GROUPS], BF16)
        nc.scalar.dma_start(out=off_sb[:], in_=offset_w)
        ws_sb = keep.tile([P, GROUPS], BF16)
        nc.scalar.dma_start(out=ws_sb[:], in_=weight_scales)
        x_bf = {}
        chunks = [[0], [1], [2], [3], [4, 5], [6, 7], [8, 9], [10, 11], [12, 13], [14, 15]]
        chunks = chunks + [[t, t + 1, t + 2, t + 3] for t in range(16, TILES, 4)]
        w_sb = keep.tile([P, FEATURES], BF16)
        for c, tiles in enumerate(chunks):
            n = len(tiles)
            xc = keep.tile([P, n, FEATURES], BF16, name="xc%d" % c)
            nc.sync.dma_start(out=xc[:], in_=x_view[:, tiles[0] : tiles[0] + n, :])
            for i, t in enumerate(tiles):
                x_bf[t] = xc[:, i, :]
            if c == 4:
                nc.sync.dma_start(out=w_sb[:], in_=weight)

        ident = keep.tile([P, P], F32)
        make_identity(nc, ident[:])

        bank_of = {}
        grouped_of = {}
        codes_of = {}

        def scale(t):
            nc.vector.tensor_scalar(out=x_bf[t], in0=x_bf[t], scalar1=s_sb[:, t : t + 1], scalar2=None, op0=ALU.mult)

        def transposes(key, src):
            bank = xb_pool.tile([P, PASSES * 2, P], F32, tag="xb")
            words = src.bitcast(F32)
            for i in range(PASSES * 2):
                nc.tensor.transpose(out=bank[:, i, :], in_=words[:, i * P : (i + 1) * P], identity=ident[:])
            bank_of[key] = bank

        def regroup(key, dst, on_vector):
            o = dst.rearrange("p (g r u) -> p g r u", g=PASSES, u=2)
            i = bank_of[key][:].rearrange("p (g u) r -> p g r u", g=PASSES)
            if on_vector:
                nc.vector.tensor_copy(out=o, in_=i)
            else:
                nc.scalar.copy(out=o, in_=i)

        def regroup_pair(j):
            grouped = work.tile([P, 2 * FEATURES], BF16, align_bytes=64)
            words = grouped[:].bitcast(F32)
            for a in range(2):
                t = 2 * j + a
                regroup(t, words[:, a * WORDS : (a + 1) * WORDS], t % 16 == 9)
            grouped_of[j] = grouped

        def quantise_pair(j, parts):
            codes = work.tile([P, 2 * PASSES * P], U32, align_bytes=64)
            scl = work.tile([P, 2 * PASSES * P], U8, align_bytes=64)
            n = 2 * PASSES * P // parts
            for a in range(parts):
                nc.vector.quantize_mx(
                    out=codes[:, a * n : (a + 1) * n].bitcast(FP8X4),
                    scales=scl[:, a * n : (a + 1) * n],
                    in_=grouped_of[j][:, 4 * a * n : 4 * (a + 1) * n],
                )
            codes_of[j] = (codes, scl)

        w_deq = keep.tile([P, FEATURES], BF16)
        w_grouped = keep.tile([P, FEATURES], BF16, align_bytes=64)
        wc = keep.tile([P, (PASSES + 1) * OUTS], U32, align_bytes=64)
        wsc = keep.tile([P, (PASSES + 1) * OUTS], U8, align_bytes=64)

        def w_dequantise():
            for q in range(GROUPS):
                nc.vector.tensor_scalar(
                    out=w_deq[:, q * P : (q + 1) * P],
                    in0=w_sb[:, q * P : (q + 1) * P],
                    scalar1=off_sb[:, q : q + 1],
                    scalar2=ws_sb[:, q : q + 1],
                    op0=ALU.subtract,
                    op1=ALU.mult,
                )

        def w_quantise():
            n = PASSES * OUTS
            nc.vector.quantize_mx(out=wc[:, 0:n].bitcast(FP8X4), scales=wsc[:, 0:n], in_=w_grouped[:])
            nc.vector.quantize_mx(out=wc[:, n:].bitcast(FP8X4), scales=wsc[:, n:], in_=w_grouped[:, 0 : 4 * OUTS])

        acc_of = {}

        def multiply(t):
            codes, scl = codes_of[t // 2]
            if t % 4 == 0 or t == TILES - 1:
                acc = acc_pool.tile([P, 4 * OUTS], F32)
            else:
                acc = acc_of[t - 1]
            acc_of[t] = acc
            slot = t % 4
            width = 2 * OUTS if t % 2 == 0 else OUTS
            for g in range(PASSES):
                cols = slice((t % 2 * PASSES + g) * P, (t % 2 * PASSES + g + 1) * P)
                w_cols = slice(g * OUTS, g * OUTS + width)
                nc.tensor.matmul_mx(
                    out=acc[:, slot * OUTS : slot * OUTS + width],
                    lhsT=codes[:, cols].bitcast(FP8X4),
                    lhsT_scale=scl[:, cols],
                    rhs=wc[:, w_cols].bitcast(FP8X4),
                    rhs_scale=wsc[:, w_cols],
                    start=(g == 0),
                    stop=(g == PASSES - 1),
                )

        results = keep.tile([P, TILES, OUTS], F32)
        store_ends = [16, 32, 48, 56, 60, 63, 64]

        def send(t0, t1):
            slot = t0 % 4
            nc.scalar.copy(
                out=results[:, t0:t1, :].rearrange("p t o -> p (t o)"),
                in_=acc_of[t0][:, slot * OUTS : (slot + t1 - t0) * OUTS],
            )
            if t1 in store_ends:
                first = max([0] + [e for e in store_ends if e < t1])
                nc.sync.dma_start(out=out_view[:, first:t1, :], in_=results[:, first:t1, :])

        multiplied = 0
        for t in range(4):
            scale(t)
        for i in range(PAIRS + 4):
            if i == 1:
                w_dequantise()
            if 2 <= i < PAIRS + 2:
                quantise_pair(i - 2, 2 if i - 2 == PAIRS - 1 else 1)
            if i + 2 < PAIRS:
                scale(2 * i + 4)
                scale(2 * i + 5)
            if i < PAIRS:
                transposes(2 * i, x_bf[2 * i])
                transposes(2 * i + 1, x_bf[2 * i + 1])
                regroup_pair(i)
            if i == 2:
                transposes("w", w_deq[:])
                regroup("w", w_grouped[:].bitcast(F32), False)
            if i == 3:
                w_quantise()
            while multiplied < PAIRS and multiplied <= i - (5 - (i >= 12) - (i >= 20)):
                j = multiplied
                for a in range(2):
                    multiply(2 * j + a)
                    if j == PAIRS - 1:
                        send(*((TILES - 4, TILES - 1) if a == 0 else (TILES - 1, TILES)))
                if j % 2 == 1 and j < PAIRS - 1:
                    send(2 * j - 2, 2 * j + 2)
                multiplied += 1
